import numpy as np
import ml_dtypes


def mxq(x, axis, fmt="e4m3"):
    dtype, down = {"e4m3": (ml_dtypes.float8_e4m3fn, 7), "e5m2": (ml_dtypes.float8_e5m2, 14)}[fmt]
    v = np.moveaxis(np.asarray(x, np.float32).astype(ml_dtypes.bfloat16).astype(np.float64), axis, -1)
    blocks = v.reshape(v.shape[:-1] + (-1, 32))
    amax = np.abs(blocks).max(-1, keepdims=True)
    byte = np.maximum(np.where(amax > 0, np.frexp(amax)[1] - 1 + 127, 0) - down, 1)
    scale = np.exp2(byte - 127.0)
    codes = (blocks / scale).astype(np.float32).astype(dtype).astype(np.float64)
    return np.moveaxis((codes * scale).reshape(v.shape), -1, axis)


WIDE = False


def mx_kscale(k):
    if not WIDE:
        return np.ones(k)
    levels = np.array([10, -10, 5, -5, 0])
    a = np.random.permutation(np.resize(levels, k // 512 * 4)).reshape(k // 512, 4)
    idx = np.arange(k)
    return np.exp2(a[idx // 512, idx % 128 // 32])


BF16 = ml_dtypes.bfloat16


def bf(x):
    return np.asarray(x, np.float32).astype(BF16)


def f64(x):
    return np.asarray(x).astype(np.float64)


B, S, D, W = 1, 4096, 128, 512
NB = S // W
MASK_VALUE = -3.4028234663852886e38


def with_prev(cur, prev, op):
    return np.concatenate([cur[:, :1], op(cur[:, 1:], prev)], axis=1)


def setup_inputs():
    t = mx_kscale(W)
    top = t.max()
    f = np.concatenate([np.full(W, top), np.tile(t, NB - 1)])
    q = np.random.standard_normal((B, S, D)) * 2.0
    k = np.random.standard_normal((B, S, D))
    v = np.random.standard_normal((B, S, D)) * (top / f)[:, None]
    q[..., 0] = 8.0
    k[..., 0] += np.log(f) / (8.0 * D ** -0.5)
    return {"q": bf(q), "k": bf(k), "v": bf(v)}


def reference(q, k, v):
    scale = D ** -0.5
    qb = f64(q).reshape(B, NB, W, D)
    kt = f64(k).reshape(B, NB, W, D).transpose(0, 1, 3, 2)
    vq = mxq(f64(v).reshape(B, NB, W, D), 2, "e4m3")
    a = np.arange(W)[:, None]
    c = np.arange(W)[None, :]
    sc = np.where(c <= a, qb @ kt * scale, MASK_VALUE)
    sp = np.where(c > a, qb[:, 1:] @ kt[:, :-1] * scale, MASK_VALUE)
    m = with_prev(sc.max(-1, keepdims=True), sp.max(-1, keepdims=True), np.maximum)
    ec = np.exp(sc - m)
    ep = np.exp(sp - m[:, 1:])
    num = with_prev(mxq(ec, 3, "e4m3") @ vq, mxq(ep, 3, "e4m3") @ vq[:, :-1], np.add)
    den = with_prev(ec.sum(-1, keepdims=True), ep.sum(-1, keepdims=True), np.add)
    return (num / den).reshape(B, S, D)

@@ -1,0 +1,223 @@
+from contextlib import ExitStack
+
+import concourse.mybir as mybir
+from concourse.masks import make_identity
+
+F32 = mybir.dt.float32
+BF16 = mybir.dt.bfloat16
+U32 = mybir.dt.uint32
+U8 = mybir.dt.uint8
+FP8X4 = mybir.dt.float8_e4m3fn_x4
+ALU = mybir.AluOpType
+ACT = mybir.ActivationFunctionType
+AXIS = mybir.AxisListType
+
+P = 128
+S = 4096
+D = 128
+PACK = 4
+BLOCK = PACK * P
+TILES = S // P
+BLOCKS = S // BLOCK
+SCALE = D ** -0.5
+MASKED = -3.0e38
+
+FLOPS = 2 * (2 * BLOCKS - 1) * 2 * BLOCK * BLOCK * D
+
+
+def tile_exactslidingwindowattention_kernel(tc, q, k, v, out):
+    nc = tc.nc
+    q_blocks = q.flatten_outer_dims().rearrange("(n t p) d -> n p t d", t=PACK, p=P)
+    k_blocks = k.flatten_outer_dims().rearrange("(n t p) d -> n p t d", t=PACK, p=P)
+    v_blocks = v.flatten_outer_dims().rearrange("(n t p) d -> n p t d", t=PACK, p=P)
+    out_blocks = out.flatten_outer_dims().rearrange("(n t p) d -> n p t d", t=PACK, p=P)
+
+    with ExitStack() as ctx:
+        keep = ctx.enter_context(tc.tile_pool(name="keep", bufs=1))
+        work = ctx.enter_context(tc.tile_pool(name="work", bufs=3))
+        small = ctx.enter_context(tc.tile_pool(name="small", bufs=4))
+        psum_window = ctx.enter_context(tc.psum_pool(name="psum_window", bufs=2))
+        psum_diag = ctx.enter_context(tc.psum_pool(name="psum_diag", bufs=2))
+        psum_eT = ctx.enter_context(tc.psum_pool(name="psum_eT", bufs=2))
+        psum_num = ctx.enter_context(tc.psum_pool(name="psum_num", bufs=1))
+        psum_qkT = ctx.enter_context(tc.psum_pool(name="psum_qkT", bufs=1))
+
+        q_sb = keep.tile([P, BLOCKS, PACK, D], BF16)
+        k_sb = keep.tile([P, BLOCKS, PACK, D], BF16)
+        v_sb = keep.tile([P, BLOCKS, PACK, D], BF16)
+        for n in range(BLOCKS):
+            nc.sync.dma_start(out=k_sb[:, n], in_=k_blocks[n])
+            nc.sync.dma_start(out=q_sb[:, n], in_=q_blocks[n])
+            nc.sync.dma_start(out=v_sb[:, n], in_=v_blocks[n])
+
+        ident = keep.tile([P, P], BF16)
+        make_identity(nc, ident[:])
+        mask_own_f32 = keep.tile([P, P], F32)
+        nc.gpsimd.memset(mask_own_f32[:], 0.0)
+        nc.gpsimd.affine_select(
+            out=mask_own_f32[:], in_=mask_own_f32[:], compare_op=ALU.is_ge, fill=MASKED,
+            base=0, pattern=[[-1, P]], channel_multiplier=1,
+        )
+        mask_prev_f32 = keep.tile([P, P], F32)
+        nc.gpsimd.memset(mask_prev_f32[:], 0.0)
+        nc.gpsimd.affine_select(
+            out=mask_prev_f32[:], in_=mask_prev_f32[:], compare_op=ALU.is_ge, fill=MASKED,
+            base=-1, pattern=[[1, P]], channel_multiplier=-1,
+        )
+        mask_own = keep.tile([P, P], BF16)
+        nc.vector.tensor_copy(out=mask_own[:], in_=mask_own_f32[:])
+        mask_prev = keep.tile([P, P], BF16)
+        nc.vector.tensor_copy(out=mask_prev[:], in_=mask_prev_f32[:])
+
+        grouped = []
+        for r in range(PACK):
+            grouped_r = keep.tile([P, 2, P, PACK], BF16, name="grouped%d" % r, align_bytes=64)
+            nc.vector.memset(grouped_r[:], 0.0)
+            grouped.append(grouped_r)
+
+        qT = keep.tile([D, S], BF16)
+        kT = keep.tile([D, S], BF16)
+        v_codes = keep.tile([P, BLOCKS, D], U32, align_bytes=64)
+        v_scales = keep.tile([P, BLOCKS, D], U8, align_bytes=64)
+
+        diag_ps = {}
+        diag_max = {}
+        den_parts = {}
+        num_ps = {}
+        e_sb = {}
+        e_codes = {}
+        e_scales = {}
+
+        def first_key_tile(T):
+            return max(T - PACK, 0)
+
+        def prepare(n):
+            qkT_ps = psum_qkT.tile([D, 2 * PACK, P], BF16)
+            for t in range(PACK):
+                nc.tensor.transpose(qkT_ps[:, t, :], q_sb[:, n, t, :], ident[:])
+            for t in range(PACK):
+                nc.tensor.transpose(qkT_ps[:, PACK + t, :], k_sb[:, n, t, :], ident[:])
+            cols = slice(n * BLOCK, (n + 1) * BLOCK)
+            nc.vector.tensor_copy(
+                out=qT[:, cols], in_=qkT_ps[:, 0:PACK, :].rearrange("d t p -> d (t p)"))
+            nc.vector.tensor_copy(
+                out=kT[:, cols], in_=qkT_ps[:, PACK:, :].rearrange("d t p -> d (t p)"))
+            v_grouped = work.tile([P, D, PACK], BF16, align_bytes=64)
+            nc.vector.tensor_copy(out=v_grouped[:], in_=v_sb[:, n].rearrange("p t d -> p d t"))
+            nc.vector.quantize_mx(
+                out=v_codes[:, n, :].bitcast(FP8X4),
+                scales=v_scales[:, n, :],
+                in_=v_grouped[:].rearrange("p d t -> p (d t)"),
+            )
+
+        def diagonal(n):
+            diag_ps[n] = psum_diag.tile([P, PACK, P], F32, name="diag_ps")
+            for r in range(PACK):
+                tile_cols = slice((n * PACK + r) * P, (n * PACK + r + 1) * P)
+                nc.tensor.matmul(out=diag_ps[n][:, r, :], lhsT=qT[:, tile_cols],
+                                 rhs=kT[:, tile_cols], start=True, stop=False)
+                nc.tensor.matmul(out=diag_ps[n][:, r, :], lhsT=ident[:], rhs=mask_own[:],
+                                 start=False, stop=True)
+            diag_max[n] = small.tile([P, PACK], F32, name="diag_max")
+            nc.vector.tensor_reduce(out=diag_max[n][:], in_=diag_ps[n][:], axis=AXIS.X, op=ALU.max)
+            den_parts[n] = small.tile([P, PACK, 2], F32, name="den_parts")
+            nc.vector.memset(den_parts[n][:], 0.0)
+
+        def scores(T):
+            n, r = divmod(T, PACK)
+            earlier = T - first_key_tile(T)
+            width = earlier * P
+            neg_max = small.tile([P, 1], F32)
+            e_sb[T] = work.tile([P, (PACK + 1) * P], BF16, name="e_sb")
+            if earlier > 0:
+                window_ps = psum_window.tile([P, BLOCK], F32)
+                clipped = T >= PACK
+                nc.tensor.matmul(out=window_ps[:, 0:width], lhsT=qT[:, T * P:(T + 1) * P],
+                                 rhs=kT[:, first_key_tile(T) * P:T * P],
+                                 start=True, stop=not clipped)
+                if clipped:
+                    nc.tensor.matmul(out=window_ps[:, 0:P], lhsT=ident[:], rhs=mask_prev[:],
+                                     start=False, stop=True)
+                window_max = small.tile([P, 1], F32)
+                nc.vector.tensor_reduce(out=window_max[:], in_=window_ps[:, 0:width],
+                                        axis=AXIS.X, op=ALU.max)
+                nc.vector.tensor_scalar(out=neg_max[:], in0=window_max[:],
+                                        scalar1=diag_max[n][:, r:r + 1], scalar2=-SCALE,
+                                        op0=ALU.max, op1=ALU.mult)
+                nc.scalar.activation(out=e_sb[T][:, 0:width], in_=window_ps[:, 0:width],
+                                     func=ACT.Exp, bias=neg_max[:], scale=SCALE,
+                                     accum_out=den_parts[n][:, r, 0:1])
+            else:
+                nc.vector.tensor_scalar(out=neg_max[:], in0=diag_max[n][:, r:r + 1],
+                                        scalar1=-SCALE, scalar2=None, op0=ALU.mult)
+            nc.scalar.activation(out=e_sb[T][:, width:width + P], in_=diag_ps[n][:, r, :],
+                                 func=ACT.Exp, bias=neg_max[:], scale=SCALE,
+                                 accum_out=den_parts[n][:, r, 1:2])
+
+        def transposed(T):
+            n, r = divmod(T, PACK)
+            seen = T - first_key_tile(T) + 1
+            eT_ps = psum_eT.tile([P, PACK + 1, P], BF16)
+            for j in range(seen):
+                nc.tensor.transpose(eT_ps[:, j, :], e_sb[T][:, j * P:(j + 1) * P], ident[:])
+            from_prev = seen - (r + 1)
+            if from_prev > 0:
+                nc.scalar.copy(out=grouped[r][:, 0, :, r:PACK],
+                               in_=eT_ps[:, 0:from_prev, :].rearrange("p t q -> p q t"))
+            nc.scalar.copy(out=grouped[r][:, 1, :, 0:r + 1],
+                           in_=eT_ps[:, from_prev:seen, :].rearrange("p t q -> p q t"))
+
+        def quantised(T):
+            n, r = divmod(T, PACK)
+            first_side = 0 if n > 0 else 1
+            e_codes[T] = work.tile([P, 2 * P], U32, name="e_codes", align_bytes=64)
+            e_scales[T] = work.tile([P, 2 * P], U8, name="e_scales", align_bytes=64)
+            nc.vector.quantize_mx(
+                out=e_codes[T][:, first_side * P:].bitcast(FP8X4),
+                scales=e_scales[T][:, first_side * P:],
+                in_=grouped[r][:, first_side:, :, :].rearrange("p s q t -> p (s q t)"),
+            )
+
+        def product(T):
+            n, r = divmod(T, PACK)
+            if r == 0:
+                num_ps[n] = psum_num.tile([P, PACK, D], F32, name="num_ps")
+            first_side = 0 if n > 0 else 1
+            for side in range(first_side, 2):
+                cols = slice(side * P, (side + 1) * P)
+                nc.tensor.matmul_mx(
+                    out=num_ps[n][:, r, :],
+                    lhsT=e_codes[T][:, cols].bitcast(FP8X4),
+                    lhsT_scale=e_scales[T][:, cols],
+                    rhs=v_codes[:, n - 1 + side, :].bitcast(FP8X4),
+                    rhs_scale=v_scales[:, n - 1 + side, :],
+                    start=(side == first_side),
+                    stop=(side == 1),
+                )
+            if r == PACK - 1:
+                den = small.tile([P, PACK], F32)
+                nc.vector.tensor_reduce(out=den[:], in_=den_parts[n][:], axis=AXIS.X, op=ALU.add)
+                inv_den = small.tile([P, PACK], F32)
+                nc.vector.reciprocal(out=inv_den[:], in_=den[:])
+                out_sb = work.tile([P, PACK, D], F32)
+                nc.vector.tensor_tensor(out=out_sb[:], in0=num_ps[n][:],
+                                        in1=inv_den[:].unsqueeze(2).to_broadcast([P, PACK, D]),
+                                        op=ALU.mult)
+                nc.sync.dma_start(out=out_blocks[n], in_=out_sb[:])
+
+        prepare(0)
+        diagonal(0)
+        for step in range(TILES + 3):
+            n, r = divmod(step, PACK)
+            if step < TILES:
+                scores(step)
+            if r == 2 and n + 1 < BLOCKS:
+                diagonal(n + 1)
+            if 0 <= step - 1 < TILES:
+                transposed(step - 1)
+            if r == 0 and n + 1 < BLOCKS:
+                prepare(n + 1)
+            if 0 <= step - 2 < TILES:
+                quantised(step - 2)
+            if 0 <= step - 3 < TILES:
+                product(step - 3)

@@ -29,12 +29,14 @@ def tile_exactslidingwindowattention_kernel(tc, q, k, v, out):
     nc = tc.nc
     q_blocks = q.flatten_outer_dims().rearrange("(n t p) d -> n p t d", t=PACK, p=P)
     k_blocks = k.flatten_outer_dims().rearrange("(n t p) d -> n p t d", t=PACK, p=P)
-    v_blocks = v.flatten_outer_dims().rearrange("(n t p) d -> n p t d", t=PACK, p=P)
+    v_blocks = v.flatten_outer_dims().rearrange("(n u p e) d -> n p u (e d)", u=2, p=P, e=2)
     out_blocks = out.flatten_outer_dims().rearrange("(n t p) d -> n p t d", t=PACK, p=P)
 
     with ExitStack() as ctx:
+        ctx.enter_context(tc.manual_schedule())
         keep = ctx.enter_context(tc.tile_pool(name="keep", bufs=1))
-        work = ctx.enter_context(tc.tile_pool(name="work", bufs=3))
+        work = ctx.enter_context(tc.tile_pool(name="work", bufs=4))
+        per_block = ctx.enter_context(tc.tile_pool(name="per_block", bufs=2))
         small = ctx.enter_context(tc.tile_pool(name="small", bufs=4))
         psum_window = ctx.enter_context(tc.psum_pool(name="psum_window", bufs=2))
         psum_diag = ctx.enter_context(tc.psum_pool(name="psum_diag", bufs=2))
@@ -45,13 +47,22 @@ def tile_exactslidingwindowattention_kernel(tc, q, k, v, out):
         q_sb = keep.tile([P, BLOCKS, PACK, D], BF16)
         k_sb = keep.tile([P, BLOCKS, PACK, D], BF16)
         v_sb = keep.tile([P, BLOCKS, PACK, D], BF16)
+
+        def load_v(n):
+            nc.sync.dma_start(out=v_sb[:, n].rearrange("p (u e) d -> p u (e d)", u=2),
+                              in_=v_blocks[n])
+
         for n in range(BLOCKS):
             nc.sync.dma_start(out=k_sb[:, n], in_=k_blocks[n])
             nc.sync.dma_start(out=q_sb[:, n], in_=q_blocks[n])
-            nc.sync.dma_start(out=v_sb[:, n], in_=v_blocks[n])
+            if n > 0:
+                load_v(n - 1)
+        load_v(BLOCKS - 1)
 
         ident = keep.tile([P, P], BF16)
         make_identity(nc, ident[:])
+        ident_f32 = keep.tile([P, P], F32)
+        make_identity(nc, ident_f32[:])
         mask_own_f32 = keep.tile([P, P], F32)
         nc.gpsimd.memset(mask_own_f32[:], 0.0)
         nc.gpsimd.affine_select(
@@ -69,11 +80,11 @@ def tile_exactslidingwindowattention_kernel(tc, q, k, v, out):
         mask_prev = keep.tile([P, P], BF16)
         nc.vector.tensor_copy(out=mask_prev[:], in_=mask_prev_f32[:])
 
-        grouped = []
+        e_win = []
         for r in range(PACK):
-            grouped_r = keep.tile([P, 2, P, PACK], BF16, name="grouped%d" % r, align_bytes=64)
-            nc.vector.memset(grouped_r[:], 0.0)
-            grouped.append(grouped_r)
+            e_win_r = keep.tile([P, 2 * BLOCK], BF16, name="e_win%d" % r)
+            nc.vector.memset(e_win_r[:], 0.0)
+            e_win.append(e_win_r)
 
         qT = keep.tile([D, S], BF16)
         kT = keep.tile([D, S], BF16)
@@ -82,26 +93,30 @@ def tile_exactslidingwindowattention_kernel(tc, q, k, v, out):
 
         diag_ps = {}
         diag_max = {}
+        window_ps = {}
         den_parts = {}
         num_ps = {}
-        e_sb = {}
+        grouped = {}
         e_codes = {}
         e_scales = {}
 
         def first_key_tile(T):
             return max(T - PACK, 0)
 
-        def prepare(n):
+        def first_side(n):
+            return 0 if n > 0 else 1
+
+        def prepare_qk(n):
             qkT_ps = psum_qkT.tile([D, 2 * PACK, P], BF16)
             for t in range(PACK):
-                nc.tensor.transpose(qkT_ps[:, t, :], q_sb[:, n, t, :], ident[:])
+                nc.tensor.transpose(qkT_ps[:, t, :], k_sb[:, n, t, :], ident[:])
             for t in range(PACK):
-                nc.tensor.transpose(qkT_ps[:, PACK + t, :], k_sb[:, n, t, :], ident[:])
+                nc.tensor.transpose(qkT_ps[:, PACK + t, :], q_sb[:, n, t, :], ident[:])
             cols = slice(n * BLOCK, (n + 1) * BLOCK)
-            nc.vector.tensor_copy(
-                out=qT[:, cols], in_=qkT_ps[:, 0:PACK, :].rearrange("d t p -> d (t p)"))
-            nc.vector.tensor_copy(
-                out=kT[:, cols], in_=qkT_ps[:, PACK:, :].rearrange("d t p -> d (t p)"))
+            nc.scalar.copy(out=kT[:, cols], in_=qkT_ps[:, 0:PACK, :].rearrange("d t p -> d (t p)"))
+            nc.scalar.copy(out=qT[:, cols], in_=qkT_ps[:, PACK:, :].rearrange("d t p -> d (t p)"))
+
+        def prepare_v(n):
             v_grouped = work.tile([P, D, PACK], BF16, align_bytes=64)
             nc.vector.tensor_copy(out=v_grouped[:], in_=v_sb[:, n].rearrange("p t d -> p d t"))
             nc.vector.quantize_mx(
@@ -110,7 +125,7 @@ def tile_exactslidingwindowattention_kernel(tc, q, k, v, out):
                 in_=v_grouped[:].rearrange("p d t -> p (d t)"),
             )
 
-        def diagonal(n):
+        def diagonal_scores(n):
             diag_ps[n] = psum_diag.tile([P, PACK, P], F32, name="diag_ps")
             for r in range(PACK):
                 tile_cols = slice((n * PACK + r) * P, (n * PACK + r + 1) * P)
@@ -118,106 +133,126 @@ def tile_exactslidingwindowattention_kernel(tc, q, k, v, out):
                                  rhs=kT[:, tile_cols], start=True, stop=False)
                 nc.tensor.matmul(out=diag_ps[n][:, r, :], lhsT=ident[:], rhs=mask_own[:],
                                  start=False, stop=True)
+
+        def diagonal_max(n):
             diag_max[n] = small.tile([P, PACK], F32, name="diag_max")
             nc.vector.tensor_reduce(out=diag_max[n][:], in_=diag_ps[n][:], axis=AXIS.X, op=ALU.max)
             den_parts[n] = small.tile([P, PACK, 2], F32, name="den_parts")
-            nc.vector.memset(den_parts[n][:], 0.0)
+            nc.gpsimd.memset(den_parts[n][:], 0.0)
 
-        def scores(T):
+        def window_scores(T):
+            if T == 0:
+                return
+            window_ps[T] = psum_window.tile([P, BLOCK], F32, name="window_ps")
+            clipped = T >= PACK
+            nc.tensor.matmul(out=window_ps[T][:, 0:(T - first_key_tile(T)) * P],
+                             lhsT=qT[:, T * P:(T + 1) * P],
+                             rhs=kT[:, first_key_tile(T) * P:T * P],
+                             start=True, stop=not clipped)
+            if clipped:
+                nc.tensor.matmul(out=window_ps[T][:, 0:P], lhsT=ident[:], rhs=mask_prev[:],
+                                 start=False, stop=True)
+
+        def softmax(T):
             n, r = divmod(T, PACK)
-            earlier = T - first_key_tile(T)
-            width = earlier * P
+            width = (T - first_key_tile(T)) * P
+            base = (first_key_tile(T) - (n - 1) * PACK) * P
             neg_max = small.tile([P, 1], F32)
-            e_sb[T] = work.tile([P, (PACK + 1) * P], BF16, name="e_sb")
-            if earlier > 0:
-                window_ps = psum_window.tile([P, BLOCK], F32)
-                clipped = T >= PACK
-                nc.tensor.matmul(out=window_ps[:, 0:width], lhsT=qT[:, T * P:(T + 1) * P],
-                                 rhs=kT[:, first_key_tile(T) * P:T * P],
-                                 start=True, stop=not clipped)
-                if clipped:
-                    nc.tensor.matmul(out=window_ps[:, 0:P], lhsT=ident[:], rhs=mask_prev[:],
-                                     start=False, stop=True)
+            if T > 0:
                 window_max = small.tile([P, 1], F32)
-                nc.vector.tensor_reduce(out=window_max[:], in_=window_ps[:, 0:width],
+                nc.vector.tensor_reduce(out=window_max[:], in_=window_ps[T][:, 0:width],
                                         axis=AXIS.X, op=ALU.max)
                 nc.vector.tensor_scalar(out=neg_max[:], in0=window_max[:],
                                         scalar1=diag_max[n][:, r:r + 1], scalar2=-SCALE,
                                         op0=ALU.max, op1=ALU.mult)
-                nc.scalar.activation(out=e_sb[T][:, 0:width], in_=window_ps[:, 0:width],
+                nc.scalar.activation(out=e_win[r][:, base:base + width],
+                                     in_=window_ps[T][:, 0:width],
                                      func=ACT.Exp, bias=neg_max[:], scale=SCALE,
                                      accum_out=den_parts[n][:, r, 0:1])
             else:
                 nc.vector.tensor_scalar(out=neg_max[:], in0=diag_max[n][:, r:r + 1],
                                         scalar1=-SCALE, scalar2=None, op0=ALU.mult)
-            nc.scalar.activation(out=e_sb[T][:, width:width + P], in_=diag_ps[n][:, r, :],
+            nc.scalar.activation(out=e_win[r][:, base + width:base + width + P],
+                                 in_=diag_ps[n][:, r, :],
                                  func=ACT.Exp, bias=neg_max[:], scale=SCALE,
                                  accum_out=den_parts[n][:, r, 1:2])
 
         def transposed(T):
             n, r = divmod(T, PACK)
-            seen = T - first_key_tile(T) + 1
-            eT_ps = psum_eT.tile([P, PACK + 1, P], BF16)
-            for j in range(seen):
-                nc.tensor.transpose(eT_ps[:, j, :], e_sb[T][:, j * P:(j + 1) * P], ident[:])
-            from_prev = seen - (r + 1)
-            if from_prev > 0:
-                nc.scalar.copy(out=grouped[r][:, 0, :, r:PACK],
-                               in_=eT_ps[:, 0:from_prev, :].rearrange("p t q -> p q t"))
-            nc.scalar.copy(out=grouped[r][:, 1, :, 0:r + 1],
-                           in_=eT_ps[:, from_prev:seen, :].rearrange("p t q -> p q t"))
+            eT_ps = psum_eT.tile([P, 2, 2, P], F32)
+            words = e_win[r][:].bitcast(F32)
+            for side in range(first_side(n), 2):
+                for u in range(2):
+                    c = (2 * side + u) * P
+                    nc.tensor.transpose(eT_ps[:, side, u, :], words[:, c:c + P], ident_f32[:])
+            grouped[T] = work.tile([P, 2, P, PACK], BF16, name="grouped", align_bytes=64)
+            nc.scalar.copy(
+                out=grouped[T][:].rearrange("p s q t -> p (s q t)").bitcast(F32).rearrange(
+                    "p (s q u) -> p s q u", s=2, u=2)[:, first_side(n):],
+                in_=eT_ps[:, first_side(n):].rearrange("p s u q -> p s q u"))
 
         def quantised(T):
             n, r = divmod(T, PACK)
-            first_side = 0 if n > 0 else 1
-            e_codes[T] = work.tile([P, 2 * P], U32, name="e_codes", align_bytes=64)
-            e_scales[T] = work.tile([P, 2 * P], U8, name="e_scales", align_bytes=64)
+            if r == 0:
+                e_codes[n] = per_block.tile([P, PACK, 2 * P], U32, name="e_codes", align_bytes=64)
+                e_scales[n] = per_block.tile([P, PACK, 2 * P], U8, name="e_scales", align_bytes=64)
             nc.vector.quantize_mx(
-                out=e_codes[T][:, first_side * P:].bitcast(FP8X4),
-                scales=e_scales[T][:, first_side * P:],
-                in_=grouped[r][:, first_side:, :, :].rearrange("p s q t -> p (s q t)"),
+                out=e_codes[n][:, r, first_side(n) * P:].bitcast(FP8X4),
+                scales=e_scales[n][:, r, first_side(n) * P:],
+                in_=grouped[T][:, first_side(n):, :, :].rearrange("p s q t -> p (s q t)"),
             )
 
-        def product(T):
-            n, r = divmod(T, PACK)
-            if r == 0:
-                num_ps[n] = psum_num.tile([P, PACK, D], F32, name="num_ps")
-            first_side = 0 if n > 0 else 1
-            for side in range(first_side, 2):
-                cols = slice(side * P, (side + 1) * P)
-                nc.tensor.matmul_mx(
-                    out=num_ps[n][:, r, :],
-                    lhsT=e_codes[T][:, cols].bitcast(FP8X4),
-                    lhsT_scale=e_scales[T][:, cols],
-                    rhs=v_codes[:, n - 1 + side, :].bitcast(FP8X4),
-                    rhs_scale=v_scales[:, n - 1 + side, :],
-                    start=(side == first_side),
-                    stop=(side == 1),
-                )
-            if r == PACK - 1:
-                den = small.tile([P, PACK], F32)
-                nc.vector.tensor_reduce(out=den[:], in_=den_parts[n][:], axis=AXIS.X, op=ALU.add)
-                inv_den = small.tile([P, PACK], F32)
-                nc.vector.reciprocal(out=inv_den[:], in_=den[:])
-                out_sb = work.tile([P, PACK, D], F32)
-                nc.vector.tensor_tensor(out=out_sb[:], in0=num_ps[n][:],
-                                        in1=inv_den[:].unsqueeze(2).to_broadcast([P, PACK, D]),
-                                        op=ALU.mult)
-                nc.sync.dma_start(out=out_blocks[n], in_=out_sb[:])
+        def product(n):
+            num_ps[n] = psum_num.tile([P, PACK, D], F32, name="num_ps")
+            for r in range(PACK):
+                for side in range(first_side(n), 2):
+                    cols = slice(side * P, (side + 1) * P)
+                    nc.tensor.matmul_mx(
+                        out=num_ps[n][:, r, :],
+                        lhsT=e_codes[n][:, r, cols].bitcast(FP8X4),
+                        lhsT_scale=e_scales[n][:, r, cols],
+                        rhs=v_codes[:, n - 1 + side, :].bitcast(FP8X4),
+                        rhs_scale=v_scales[:, n - 1 + side, :],
+                        start=(side == first_side(n)),
+                        stop=(side == 1),
+                    )
 
-        prepare(0)
-        diagonal(0)
-        for step in range(TILES + 3):
+        def normalised(n):
+            den = small.tile([P, PACK], F32)
+            nc.vector.tensor_reduce(out=den[:], in_=den_parts[n][:], axis=AXIS.X, op=ALU.add)
+            inv_den = small.tile([P, PACK], F32)
+            nc.vector.reciprocal(out=inv_den[:], in_=den[:])
+            out_sb = per_block.tile([P, PACK, D], F32)
+            nc.vector.tensor_tensor(out=out_sb[:], in0=num_ps[n][:],
+                                    in1=inv_den[:].unsqueeze(2).to_broadcast([P, PACK, D]),
+                                    op=ALU.mult)
+            nc.sync.dma_start(out=out_blocks[n], in_=out_sb[:])
+
+        def in_range(x, count):
+            return 0 <= x < count
+
+        prepare_qk(0)
+        diagonal_scores(0)
+        diagonal_max(0)
+        for step in range(-1, TILES + 2 * PACK + 1):
             n, r = divmod(step, PACK)
-            if step < TILES:
-                scores(step)
-            if r == 2 and n + 1 < BLOCKS:
-                diagonal(n + 1)
-            if 0 <= step - 1 < TILES:
+            if in_range(step + 1, TILES):
+                window_scores(step + 1)
+            if in_range(step, TILES):
+                softmax(step)
+            if in_range(step - 1, TILES):
                 transposed(step - 1)
-            if r == 0 and n + 1 < BLOCKS:
-                prepare(n + 1)
-            if 0 <= step - 2 < TILES:
-                quantised(step - 2)
-            if 0 <= step - 3 < TILES:
-                product(step - 3)
+            if in_range(step - 3, TILES):
+                quantised(step - 3)
+            if r == 0 and in_range(n + 1, BLOCKS):
+                prepare_qk(n + 1)
+            if r == 0 and in_range(n - 2, BLOCKS):
+                normalised(n - 2)
+            if r == 1 and in_range(n + 1, BLOCKS):
+                diagonal_scores(n + 1)
+            if r == 2 and in_range(n + 1, BLOCKS):
+                diagonal_max(n + 1)
+            if r == 3 and in_range(n, BLOCKS):
+                prepare_v(n)
+            if r == 3 and in_range(n - 1, BLOCKS):
+                product(n - 1)

@@ -21,6 +21,7 @@ TILES = S // P
 BLOCKS = S // BLOCK
 SCALE = D ** -0.5
 MASKED = -3.0e38
+V_GROUP = 2
 
 FLOPS = 2 * (2 * BLOCKS - 1) * 2 * BLOCK * BLOCK * D
 
@@ -29,7 +30,7 @@ def tile_exactslidingwindowattention_kernel(tc, q, k, v, out):
     nc = tc.nc
     q_blocks = q.flatten_outer_dims().rearrange("(n t p) d -> n p t d", t=PACK, p=P)
     k_blocks = k.flatten_outer_dims().rearrange("(n t p) d -> n p t d", t=PACK, p=P)
-    v_blocks = v.flatten_outer_dims().rearrange("(n u p e) d -> n p u (e d)", u=2, p=P, e=2)
+    v_runs = v.flatten_outer_dims().rearrange("(c p e) d -> p c (e d)", p=P, e=2)
     out_blocks = out.flatten_outer_dims().rearrange("(n t p) d -> n p t d", t=PACK, p=P)
 
     with ExitStack() as ctx:
@@ -37,27 +38,39 @@ def tile_exactslidingwindowattention_kernel(tc, q, k, v, out):
         keep = ctx.enter_context(tc.tile_pool(name="keep", bufs=1))
         work = ctx.enter_context(tc.tile_pool(name="work", bufs=4))
         per_block = ctx.enter_context(tc.tile_pool(name="per_block", bufs=2))
-        small = ctx.enter_context(tc.tile_pool(name="small", bufs=4))
-        psum_window = ctx.enter_context(tc.psum_pool(name="psum_window", bufs=2))
+        small = ctx.enter_context(tc.tile_pool(name="small", bufs=6))
+        psum_window = ctx.enter_context(tc.psum_pool(name="psum_window", bufs=3))
         psum_diag = ctx.enter_context(tc.psum_pool(name="psum_diag", bufs=2))
         psum_eT = ctx.enter_context(tc.psum_pool(name="psum_eT", bufs=2))
-        psum_num = ctx.enter_context(tc.psum_pool(name="psum_num", bufs=1))
-        psum_qkT = ctx.enter_context(tc.psum_pool(name="psum_qkT", bufs=1))
+        psum_turns = ctx.enter_context(tc.psum_pool(name="psum_turns", bufs=1))
 
         q_sb = keep.tile([P, BLOCKS, PACK, D], BF16)
         k_sb = keep.tile([P, BLOCKS, PACK, D], BF16)
         v_sb = keep.tile([P, BLOCKS, PACK, D], BF16)
 
-        def load_v(n):
-            nc.sync.dma_start(out=v_sb[:, n].rearrange("p (u e) d -> p u (e d)", u=2),
-                              in_=v_blocks[n])
-
-        for n in range(BLOCKS):
+        def load_qk(n):
             nc.sync.dma_start(out=k_sb[:, n], in_=k_blocks[n])
             nc.sync.dma_start(out=q_sb[:, n], in_=q_blocks[n])
-            if n > 0:
-                load_v(n - 1)
-        load_v(BLOCKS - 1)
+
+        load_qk(0)
+        load_qk(1)
+        for g in range(BLOCKS // V_GROUP):
+            nc.sync.dma_start(
+                out=v_sb[:, g * V_GROUP:(g + 1) * V_GROUP].rearrange(
+                    "p n (u e) d -> p (n u) (e d)", u=2),
+                in_=v_runs[:, 2 * g * V_GROUP:2 * (g + 1) * V_GROUP, :])
+        for n in range(2, BLOCKS):
+            load_qk(n)
+
+        e_win = []
+        for r in range(PACK):
+            e_win_r = keep.tile([P, 2 * BLOCK], BF16, name="e_win%d" % r)
+            nc.vector.memset(e_win_r[:], 0.0)
+            e_win.append(e_win_r)
+        den_parts = keep.tile([P, BLOCKS, PACK, 2], F32)
+        nc.vector.memset(den_parts[:], 0.0)
+        table_warmer = keep.tile([P, 1], F32)
+        nc.scalar.activation(out=table_warmer[:], in_=den_parts[:, 0, 0, 0:1], func=ACT.Exp)
 
         ident = keep.tile([P, P], BF16)
         make_identity(nc, ident[:])
@@ -80,25 +93,32 @@ def tile_exactslidingwindowattention_kernel(tc, q, k, v, out):
         mask_prev = keep.tile([P, P], BF16)
         nc.vector.tensor_copy(out=mask_prev[:], in_=mask_prev_f32[:])
 
-        e_win = []
-        for r in range(PACK):
-            e_win_r = keep.tile([P, 2 * BLOCK], BF16, name="e_win%d" % r)
-            nc.vector.memset(e_win_r[:], 0.0)
-            e_win.append(e_win_r)
-
-        qT = keep.tile([D, S], BF16)
-        kT = keep.tile([D, S], BF16)
+        kqT = keep.tile([D, 2, S], BF16)
+        kT = kqT[:, 0, :]
+        qT = kqT[:, 1, :]
         v_codes = keep.tile([P, BLOCKS, D], U32, align_bytes=64)
         v_scales = keep.tile([P, BLOCKS, D], U8, align_bytes=64)
 
+        v_grouped = {}
+        for g in range(BLOCKS // V_GROUP):
+            v_grouped[g] = keep.tile([P, V_GROUP, D, PACK], BF16, name="v_grouped%d" % g,
+                                     align_bytes=64)
+            nc.gpsimd.tensor_scalar(
+                out=v_grouped[g][:],
+                in0=v_sb[:, g * V_GROUP:(g + 1) * V_GROUP].rearrange("p n t d -> p n d t"),
+                scalar1=1.0, scalar2=0.0, op0=ALU.mult, op1=ALU.add)
+
+        kqT_ps = {}
         diag_ps = {}
-        diag_max = {}
+        neg_diag_max = {}
         window_ps = {}
-        den_parts = {}
-        num_ps = {}
+        neg_max = {}
+        eT_ps = {}
         grouped = {}
         e_codes = {}
         e_scales = {}
+        inv_den = {}
+        num_ps = {}
 
         def first_key_tile(T):
             return max(T - PACK, 0)
@@ -106,23 +126,23 @@ def tile_exactslidingwindowattention_kernel(tc, q, k, v, out):
         def first_side(n):
             return 0 if n > 0 else 1
 
-        def prepare_qk(n):
-            qkT_ps = psum_qkT.tile([D, 2 * PACK, P], BF16)
+        def kq_transposed(n):
+            kqT_ps[n] = psum_turns.tile([D, 2, PACK, P], BF16, name="kqT_ps", tag="turns")
             for t in range(PACK):
-                nc.tensor.transpose(qkT_ps[:, t, :], k_sb[:, n, t, :], ident[:])
+                nc.tensor.transpose(kqT_ps[n][:, 0, t, :], k_sb[:, n, t, :], ident[:])
             for t in range(PACK):
-                nc.tensor.transpose(qkT_ps[:, PACK + t, :], q_sb[:, n, t, :], ident[:])
-            cols = slice(n * BLOCK, (n + 1) * BLOCK)
-            nc.scalar.copy(out=kT[:, cols], in_=qkT_ps[:, 0:PACK, :].rearrange("d t p -> d (t p)"))
-            nc.scalar.copy(out=qT[:, cols], in_=qkT_ps[:, PACK:, :].rearrange("d t p -> d (t p)"))
+                nc.tensor.transpose(kqT_ps[n][:, 1, t, :], q_sb[:, n, t, :], ident[:])
 
-        def prepare_v(n):
-            v_grouped = work.tile([P, D, PACK], BF16, align_bytes=64)
-            nc.vector.tensor_copy(out=v_grouped[:], in_=v_sb[:, n].rearrange("p t d -> p d t"))
+        def kq_copied(n):
+            nc.vector.tensor_copy(out=kqT[:, :, n * BLOCK:(n + 1) * BLOCK],
+                                  in_=kqT_ps[n][:].rearrange("d h t p -> d h (t p)"))
+
+        def v_quantised(g):
             nc.vector.quantize_mx(
-                out=v_codes[:, n, :].bitcast(FP8X4),
-                scales=v_scales[:, n, :],
-                in_=v_grouped[:].rearrange("p d t -> p (d t)"),
+                out=v_codes[:, g * V_GROUP:(g + 1) * V_GROUP, :].rearrange(
+                    "p n d -> p (n d)").bitcast(FP8X4),
+                scales=v_scales[:, g * V_GROUP:(g + 1) * V_GROUP, :].rearrange("p n d -> p (n d)"),
+                in_=v_grouped[g][:].rearrange("p n d t -> p (n d t)"),
             )
 
         def diagonal_scores(n):
@@ -135,10 +155,11 @@ def tile_exactslidingwindowattention_kernel(tc, q, k, v, out):
                                  start=False, stop=True)
 
         def diagonal_max(n):
-            diag_max[n] = small.tile([P, PACK], F32, name="diag_max")
-            nc.vector.tensor_reduce(out=diag_max[n][:], in_=diag_ps[n][:], axis=AXIS.X, op=ALU.max)
-            den_parts[n] = small.tile([P, PACK, 2], F32, name="den_parts")
-            nc.gpsimd.memset(den_parts[n][:], 0.0)
+            diag_max = small.tile([P, PACK], F32)
+            nc.vector.tensor_reduce(out=diag_max[:], in_=diag_ps[n][:], axis=AXIS.X, op=ALU.max)
+            neg_diag_max[n] = small.tile([P, PACK], F32, name="neg_diag_max")
+            nc.vector.tensor_scalar(out=neg_diag_max[n][:], in0=diag_max[:], scalar1=-SCALE,
+                                    scalar2=None, op0=ALU.mult)
 
         def window_scores(T):
             if T == 0:
@@ -153,43 +174,49 @@ def tile_exactslidingwindowattention_kernel(tc, q, k, v, out):
                 nc.tensor.matmul(out=window_ps[T][:, 0:P], lhsT=ident[:], rhs=mask_prev[:],
                                  start=False, stop=True)
 
-        def softmax(T):
+        def row_maximum(T):
+            n, r = divmod(T, PACK)
+            if T == 0:
+                neg_max[T] = neg_diag_max[n][:, r:r + 1]
+                return
+            width = (T - first_key_tile(T)) * P
+            products = work.tile([P, BLOCK], BF16)
+            neg_max_T = small.tile([P, 1], F32)
+            nc.vector.tensor_scalar(out=products[:, 0:width], in0=window_ps[T][:, 0:width],
+                                    scalar1=-SCALE, scalar2=neg_diag_max[n][:, r:r + 1],
+                                    op0=ALU.mult, op1=ALU.min, accum_out=neg_max_T[:])
+            neg_max[T] = neg_max_T[:]
+
+        def exponentials(T):
             n, r = divmod(T, PACK)
             width = (T - first_key_tile(T)) * P
             base = (first_key_tile(T) - (n - 1) * PACK) * P
-            neg_max = small.tile([P, 1], F32)
             if T > 0:
-                window_max = small.tile([P, 1], F32)
-                nc.vector.tensor_reduce(out=window_max[:], in_=window_ps[T][:, 0:width],
-                                        axis=AXIS.X, op=ALU.max)
-                nc.vector.tensor_scalar(out=neg_max[:], in0=window_max[:],
-                                        scalar1=diag_max[n][:, r:r + 1], scalar2=-SCALE,
-                                        op0=ALU.max, op1=ALU.mult)
                 nc.scalar.activation(out=e_win[r][:, base:base + width],
                                      in_=window_ps[T][:, 0:width],
-                                     func=ACT.Exp, bias=neg_max[:], scale=SCALE,
-                                     accum_out=den_parts[n][:, r, 0:1])
-            else:
-                nc.vector.tensor_scalar(out=neg_max[:], in0=diag_max[n][:, r:r + 1],
-                                        scalar1=-SCALE, scalar2=None, op0=ALU.mult)
+                                     func=ACT.Exp, bias=neg_max[T], scale=SCALE,
+                                     accum_out=den_parts[:, n, r, 0:1])
             nc.scalar.activation(out=e_win[r][:, base + width:base + width + P],
                                  in_=diag_ps[n][:, r, :],
-                                 func=ACT.Exp, bias=neg_max[:], scale=SCALE,
-                                 accum_out=den_parts[n][:, r, 1:2])
+                                 func=ACT.Exp, bias=neg_max[T], scale=SCALE,
+                                 accum_out=den_parts[:, n, r, 1:2])
 
         def transposed(T):
             n, r = divmod(T, PACK)
-            eT_ps = psum_eT.tile([P, 2, 2, P], F32)
+            eT_ps[T] = psum_eT.tile([P, 2, 2, P], F32, name="eT_ps")
             words = e_win[r][:].bitcast(F32)
             for side in range(first_side(n), 2):
                 for u in range(2):
                     c = (2 * side + u) * P
-                    nc.tensor.transpose(eT_ps[:, side, u, :], words[:, c:c + P], ident_f32[:])
+                    nc.tensor.transpose(eT_ps[T][:, side, u, :], words[:, c:c + P], ident_f32[:])
+
+        def regrouped(T):
+            n = T // PACK
             grouped[T] = work.tile([P, 2, P, PACK], BF16, name="grouped", align_bytes=64)
             nc.scalar.copy(
                 out=grouped[T][:].rearrange("p s q t -> p (s q t)").bitcast(F32).rearrange(
                     "p (s q u) -> p s q u", s=2, u=2)[:, first_side(n):],
-                in_=eT_ps[:, first_side(n):].rearrange("p s u q -> p s q u"))
+                in_=eT_ps[T][:, first_side(n):].rearrange("p s u q -> p s q u"))
 
         def quantised(T):
             n, r = divmod(T, PACK)
@@ -202,8 +229,14 @@ def tile_exactslidingwindowattention_kernel(tc, q, k, v, out):
                 in_=grouped[T][:, first_side(n):, :, :].rearrange("p s q t -> p (s q t)"),
             )
 
+        def row_sums(n):
+            den = small.tile([P, PACK], F32)
+            nc.vector.tensor_reduce(out=den[:], in_=den_parts[:, n], axis=AXIS.X, op=ALU.add)
+            inv_den[n] = small.tile([P, PACK], F32, name="inv_den")
+            nc.vector.reciprocal(out=inv_den[n][:], in_=den[:])
+
         def product(n):
-            num_ps[n] = psum_num.tile([P, PACK, D], F32, name="num_ps")
+            num_ps[n] = psum_turns.tile([P, PACK, D], F32, name="num_ps", tag="turns")
             for r in range(PACK):
                 for side in range(first_side(n), 2):
                     cols = slice(side * P, (side + 1) * P)
@@ -218,41 +251,46 @@ def tile_exactslidingwindowattention_kernel(tc, q, k, v, out):
                     )
 
         def normalised(n):
-            den = small.tile([P, PACK], F32)
-            nc.vector.tensor_reduce(out=den[:], in_=den_parts[n][:], axis=AXIS.X, op=ALU.add)
-            inv_den = small.tile([P, PACK], F32)
-            nc.vector.reciprocal(out=inv_den[:], in_=den[:])
             out_sb = per_block.tile([P, PACK, D], F32)
             nc.vector.tensor_tensor(out=out_sb[:], in0=num_ps[n][:],
-                                    in1=inv_den[:].unsqueeze(2).to_broadcast([P, PACK, D]),
+                                    in1=inv_den[n][:].unsqueeze(2).to_broadcast([P, PACK, D]),
                                     op=ALU.mult)
             nc.sync.dma_start(out=out_blocks[n], in_=out_sb[:])
 
         def in_range(x, count):
             return 0 <= x < count
 
-        prepare_qk(0)
-        diagonal_scores(0)
-        diagonal_max(0)
-        for step in range(-1, TILES + 2 * PACK + 1):
+        FIRST_V_STEP = 3
+
+        kq_transposed(0)
+        kq_copied(0)
+        for step in range(-1, TILES + 3 * PACK):
             n, r = divmod(step, PACK)
+            if r == 0 and in_range(n, BLOCKS):
+                diagonal_max(n)
+            if in_range(step - 2, TILES):
+                transposed(step - 2)
             if in_range(step + 1, TILES):
                 window_scores(step + 1)
             if in_range(step, TILES):
-                softmax(step)
+                row_maximum(step)
+            if in_range(step - 4, TILES):
+                quantised(step - 4)
             if in_range(step - 1, TILES):
-                transposed(step - 1)
+                exponentials(step - 1)
             if in_range(step - 3, TILES):
-                quantised(step - 3)
+                regrouped(step - 3)
+            if in_range(step - FIRST_V_STEP, BLOCKS // V_GROUP):
+                v_quantised(step - FIRST_V_STEP)
             if r == 0 and in_range(n + 1, BLOCKS):
-                prepare_qk(n + 1)
-            if r == 0 and in_range(n - 2, BLOCKS):
-                normalised(n - 2)
+                kq_transposed(n + 1)
             if r == 1 and in_range(n + 1, BLOCKS):
+                kq_copied(n + 1)
+            if r == 2 and in_range(n - 1, BLOCKS):
+                row_sums(n - 1)
+            if r == 2 and in_range(n - 2, BLOCKS):
+                product(n - 2)
+            if r == 3 and in_range(n + 1, BLOCKS):
                 diagonal_scores(n + 1)
-            if r == 2 and in_range(n + 1, BLOCKS):
-                diagonal_max(n + 1)
-            if r == 3 and in_range(n, BLOCKS):
-                prepare_v(n)
-            if r == 3 and in_range(n - 1, BLOCKS):
-                product(n - 1)
+            if r == 3 and in_range(n - 2, BLOCKS):
+                normalised(n - 2)

@@ -21,7 +21,6 @@ TILES = S // P
 BLOCKS = S // BLOCK
 SCALE = D ** -0.5
 MASKED = -3.0e38
-V_GROUP = 2
 
 FLOPS = 2 * (2 * BLOCKS - 1) * 2 * BLOCK * BLOCK * D
 
@@ -30,7 +29,7 @@ def tile_exactslidingwindowattention_kernel(tc, q, k, v, out):
     nc = tc.nc
     q_blocks = q.flatten_outer_dims().rearrange("(n t p) d -> n p t d", t=PACK, p=P)
     k_blocks = k.flatten_outer_dims().rearrange("(n t p) d -> n p t d", t=PACK, p=P)
-    v_runs = v.flatten_outer_dims().rearrange("(c p e) d -> p c (e d)", p=P, e=2)
+    v_blocks = v.flatten_outer_dims().rearrange("(n u p e) d -> n p u (e d)", u=2, p=P, e=2)
     out_blocks = out.flatten_outer_dims().rearrange("(n t p) d -> n p t d", t=PACK, p=P)
 
     with ExitStack() as ctx:
@@ -38,29 +37,27 @@ def tile_exactslidingwindowattention_kernel(tc, q, k, v, out):
         keep = ctx.enter_context(tc.tile_pool(name="keep", bufs=1))
         work = ctx.enter_context(tc.tile_pool(name="work", bufs=4))
         per_block = ctx.enter_context(tc.tile_pool(name="per_block", bufs=2))
-        small = ctx.enter_context(tc.tile_pool(name="small", bufs=6))
-        psum_window = ctx.enter_context(tc.psum_pool(name="psum_window", bufs=3))
+        small = ctx.enter_context(tc.tile_pool(name="small", bufs=4))
+        psum_window = ctx.enter_context(tc.psum_pool(name="psum_window", bufs=2))
         psum_diag = ctx.enter_context(tc.psum_pool(name="psum_diag", bufs=2))
         psum_eT = ctx.enter_context(tc.psum_pool(name="psum_eT", bufs=2))
-        psum_turns = ctx.enter_context(tc.psum_pool(name="psum_turns", bufs=1))
+        psum_num = ctx.enter_context(tc.psum_pool(name="psum_num", bufs=1))
+        psum_qkT = ctx.enter_context(tc.psum_pool(name="psum_qkT", bufs=1))
 
         q_sb = keep.tile([P, BLOCKS, PACK, D], BF16)
         k_sb = keep.tile([P, BLOCKS, PACK, D], BF16)
         v_sb = keep.tile([P, BLOCKS, PACK, D], BF16)
 
-        def load_qk(n):
+        def load_v(n):
+            nc.sync.dma_start(out=v_sb[:, n].rearrange("p (u e) d -> p u (e d)", u=2),
+                              in_=v_blocks[n])
+
+        for n in range(BLOCKS):
             nc.sync.dma_start(out=k_sb[:, n], in_=k_blocks[n])
             nc.sync.dma_start(out=q_sb[:, n], in_=q_blocks[n])
-
-        load_qk(0)
-        load_qk(1)
-        for g in range(BLOCKS // V_GROUP):
-            nc.sync.dma_start(
-                out=v_sb[:, g * V_GROUP:(g + 1) * V_GROUP].rearrange(
-                    "p n (u e) d -> p (n u) (e d)", u=2),
-                in_=v_runs[:, 2 * g * V_GROUP:2 * (g + 1) * V_GROUP, :])
-        for n in range(2, BLOCKS):
-            load_qk(n)
+            if n > 0:
+                load_v(n - 1)
+        load_v(BLOCKS - 1)
 
         e_win = []
         for r in range(PACK):
@@ -69,8 +66,6 @@ def tile_exactslidingwindowattention_kernel(tc, q, k, v, out):
             e_win.append(e_win_r)
         den_parts = keep.tile([P, BLOCKS, PACK, 2], F32)
         nc.vector.memset(den_parts[:], 0.0)
-        table_warmer = keep.tile([P, 1], F32)
-        nc.scalar.activation(out=table_warmer[:], in_=den_parts[:, 0, 0, 0:1], func=ACT.Exp)
 
         ident = keep.tile([P, P], BF16)
         make_identity(nc, ident[:])
@@ -99,26 +94,18 @@ def tile_exactslidingwindowattention_kernel(tc, q, k, v, out):
         v_codes = keep.tile([P, BLOCKS, D], U32, align_bytes=64)
         v_scales = keep.tile([P, BLOCKS, D], U8, align_bytes=64)
 
-        v_grouped = {}
-        for g in range(BLOCKS // V_GROUP):
-            v_grouped[g] = keep.tile([P, V_GROUP, D, PACK], BF16, name="v_grouped%d" % g,
-                                     align_bytes=64)
-            nc.gpsimd.tensor_scalar(
-                out=v_grouped[g][:],
-                in0=v_sb[:, g * V_GROUP:(g + 1) * V_GROUP].rearrange("p n t d -> p n d t"),
-                scalar1=1.0, scalar2=0.0, op0=ALU.mult, op1=ALU.add)
-
-        kqT_ps = {}
         diag_ps = {}
-        neg_diag_max = {}
+        diag_max = {}
         window_ps = {}
+        window_max = {}
         neg_max = {}
-        eT_ps = {}
+        v_grouped = {}
+        den = {}
+        inv_den = {}
+        num_ps = {}
         grouped = {}
         e_codes = {}
         e_scales = {}
-        inv_den = {}
-        num_ps = {}
 
         def first_key_tile(T):
             return max(T - PACK, 0)
@@ -126,23 +113,24 @@ def tile_exactslidingwindowattention_kernel(tc, q, k, v, out):
         def first_side(n):
             return 0 if n > 0 else 1
 
-        def kq_transposed(n):
-            kqT_ps[n] = psum_turns.tile([D, 2, PACK, P], BF16, name="kqT_ps", tag="turns")
+        def prepare_qk(n):
+            kqT_ps = psum_qkT.tile([D, 2, PACK, P], BF16)
             for t in range(PACK):
-                nc.tensor.transpose(kqT_ps[n][:, 0, t, :], k_sb[:, n, t, :], ident[:])
+                nc.tensor.transpose(kqT_ps[:, 0, t, :], k_sb[:, n, t, :], ident[:])
             for t in range(PACK):
-                nc.tensor.transpose(kqT_ps[n][:, 1, t, :], q_sb[:, n, t, :], ident[:])
+                nc.tensor.transpose(kqT_ps[:, 1, t, :], q_sb[:, n, t, :], ident[:])
+            nc.scalar.copy(out=kqT[:, :, n * BLOCK:(n + 1) * BLOCK],
+                           in_=kqT_ps[:].rearrange("d h t p -> d h (t p)"))
 
-        def kq_copied(n):
-            nc.vector.tensor_copy(out=kqT[:, :, n * BLOCK:(n + 1) * BLOCK],
-                                  in_=kqT_ps[n][:].rearrange("d h t p -> d h (t p)"))
+        def v_regrouped(n):
+            v_grouped[n] = work.tile([P, D, PACK], BF16, name="v_grouped", align_bytes=64)
+            nc.vector.tensor_copy(out=v_grouped[n][:], in_=v_sb[:, n].rearrange("p t d -> p d t"))
 
-        def v_quantised(g):
+        def v_quantised(n):
             nc.vector.quantize_mx(
-                out=v_codes[:, g * V_GROUP:(g + 1) * V_GROUP, :].rearrange(
-                    "p n d -> p (n d)").bitcast(FP8X4),
-                scales=v_scales[:, g * V_GROUP:(g + 1) * V_GROUP, :].rearrange("p n d -> p (n d)"),
-                in_=v_grouped[g][:].rearrange("p n d t -> p (n d t)"),
+                out=v_codes[:, n, :].bitcast(FP8X4),
+                scales=v_scales[:, n, :],
+                in_=v_grouped[n][:].rearrange("p d t -> p (d t)"),
             )
 
         def diagonal_scores(n):
@@ -155,11 +143,8 @@ def tile_exactslidingwindowattention_kernel(tc, q, k, v, out):
                                  start=False, stop=True)
 
         def diagonal_max(n):
-            diag_max = small.tile([P, PACK], F32)
-            nc.vector.tensor_reduce(out=diag_max[:], in_=diag_ps[n][:], axis=AXIS.X, op=ALU.max)
-            neg_diag_max[n] = small.tile([P, PACK], F32, name="neg_diag_max")
-            nc.vector.tensor_scalar(out=neg_diag_max[n][:], in0=diag_max[:], scalar1=-SCALE,
-                                    scalar2=None, op0=ALU.mult)
+            diag_max[n] = small.tile([P, PACK], F32, name="diag_max")
+            nc.vector.tensor_reduce(out=diag_max[n][:], in_=diag_ps[n][:], axis=AXIS.X, op=ALU.max)
 
         def window_scores(T):
             if T == 0:
@@ -174,18 +159,23 @@ def tile_exactslidingwindowattention_kernel(tc, q, k, v, out):
                 nc.tensor.matmul(out=window_ps[T][:, 0:P], lhsT=ident[:], rhs=mask_prev[:],
                                  start=False, stop=True)
 
+        def window_maximum(T):
+            if T > 0:
+                window_max[T] = small.tile([P, 1], F32, name="window_max")
+                nc.vector.tensor_reduce(out=window_max[T][:],
+                                        in_=window_ps[T][:, 0:(T - first_key_tile(T)) * P],
+                                        axis=AXIS.X, op=ALU.max)
+
         def row_maximum(T):
             n, r = divmod(T, PACK)
-            if T == 0:
-                neg_max[T] = neg_diag_max[n][:, r:r + 1]
-                return
-            width = (T - first_key_tile(T)) * P
-            products = work.tile([P, BLOCK], BF16)
-            neg_max_T = small.tile([P, 1], F32)
-            nc.vector.tensor_scalar(out=products[:, 0:width], in0=window_ps[T][:, 0:width],
-                                    scalar1=-SCALE, scalar2=neg_diag_max[n][:, r:r + 1],
-                                    op0=ALU.mult, op1=ALU.min, accum_out=neg_max_T[:])
-            neg_max[T] = neg_max_T[:]
+            neg_max[T] = small.tile([P, 1], F32, name="neg_max")
+            if T > 0:
+                nc.vector.tensor_scalar(out=neg_max[T][:], in0=window_max[T][:],
+                                        scalar1=diag_max[n][:, r:r + 1], scalar2=-SCALE,
+                                        op0=ALU.max, op1=ALU.mult)
+            else:
+                nc.vector.tensor_scalar(out=neg_max[T][:], in0=diag_max[n][:, r:r + 1],
+                                        scalar1=-SCALE, scalar2=None, op0=ALU.mult)
 
         def exponentials(T):
             n, r = divmod(T, PACK)
@@ -194,29 +184,26 @@ def tile_exactslidingwindowattention_kernel(tc, q, k, v, out):
             if T > 0:
                 nc.scalar.activation(out=e_win[r][:, base:base + width],
                                      in_=window_ps[T][:, 0:width],
-                                     func=ACT.Exp, bias=neg_max[T], scale=SCALE,
+                                     func=ACT.Exp, bias=neg_max[T][:], scale=SCALE,
                                      accum_out=den_parts[:, n, r, 0:1])
             nc.scalar.activation(out=e_win[r][:, base + width:base + width + P],
                                  in_=diag_ps[n][:, r, :],
-                                 func=ACT.Exp, bias=neg_max[T], scale=SCALE,
+                                 func=ACT.Exp, bias=neg_max[T][:], scale=SCALE,
                                  accum_out=den_parts[:, n, r, 1:2])
 
         def transposed(T):
             n, r = divmod(T, PACK)
-            eT_ps[T] = psum_eT.tile([P, 2, 2, P], F32, name="eT_ps")
+            eT_ps = psum_eT.tile([P, 2, 2, P], F32)
             words = e_win[r][:].bitcast(F32)
             for side in range(first_side(n), 2):
                 for u in range(2):
                     c = (2 * side + u) * P
-                    nc.tensor.transpose(eT_ps[T][:, side, u, :], words[:, c:c + P], ident_f32[:])
-
-        def regrouped(T):
-            n = T // PACK
+                    nc.tensor.transpose(eT_ps[:, side, u, :], words[:, c:c + P], ident_f32[:])
             grouped[T] = work.tile([P, 2, P, PACK], BF16, name="grouped", align_bytes=64)
             nc.scalar.copy(
                 out=grouped[T][:].rearrange("p s q t -> p (s q t)").bitcast(F32).rearrange(
                     "p (s q u) -> p s q u", s=2, u=2)[:, first_side(n):],
-                in_=eT_ps[T][:, first_side(n):].rearrange("p s u q -> p s q u"))
+                in_=eT_ps[:, first_side(n):].rearrange("p s u q -> p s q u"))
 
         def quantised(T):
             n, r = divmod(T, PACK)
@@ -229,14 +216,8 @@ def tile_exactslidingwindowattention_kernel(tc, q, k, v, out):
                 in_=grouped[T][:, first_side(n):, :, :].rearrange("p s q t -> p (s q t)"),
             )
 
-        def row_sums(n):
-            den = small.tile([P, PACK], F32)
-            nc.vector.tensor_reduce(out=den[:], in_=den_parts[:, n], axis=AXIS.X, op=ALU.add)
-            inv_den[n] = small.tile([P, PACK], F32, name="inv_den")
-            nc.vector.reciprocal(out=inv_den[n][:], in_=den[:])
-
         def product(n):
-            num_ps[n] = psum_turns.tile([P, PACK, D], F32, name="num_ps", tag="turns")
+            num_ps[n] = psum_num.tile([P, PACK, D], F32, name="num_ps")
             for r in range(PACK):
                 for side in range(first_side(n), 2):
                     cols = slice(side * P, (side + 1) * P)
@@ -250,6 +231,14 @@ def tile_exactslidingwindowattention_kernel(tc, q, k, v, out):
                         stop=(side == 1),
                     )
 
+        def row_sums(n):
+            den[n] = small.tile([P, PACK], F32, name="den")
+            nc.vector.tensor_reduce(out=den[n][:], in_=den_parts[:, n], axis=AXIS.X, op=ALU.add)
+
+        def reciprocals(n):
+            inv_den[n] = small.tile([P, PACK], F32, name="inv_den")
+            nc.vector.reciprocal(out=inv_den[n][:], in_=den[n][:])
+
         def normalised(n):
             out_sb = per_block.tile([P, PACK, D], F32)
             nc.vector.tensor_tensor(out=out_sb[:], in0=num_ps[n][:],
@@ -260,37 +249,37 @@ def tile_exactslidingwindowattention_kernel(tc, q, k, v, out):
         def in_range(x, count):
             return 0 <= x < count
 
-        FIRST_V_STEP = 3
-
-        kq_transposed(0)
-        kq_copied(0)
-        for step in range(-1, TILES + 3 * PACK):
+        prepare_qk(0)
+        diagonal_scores(0)
+        diagonal_max(0)
+        for step in range(-1, TILES + 2 * PACK + 1):
             n, r = divmod(step, PACK)
-            if r == 0 and in_range(n, BLOCKS):
-                diagonal_max(n)
-            if in_range(step - 2, TILES):
-                transposed(step - 2)
             if in_range(step + 1, TILES):
                 window_scores(step + 1)
             if in_range(step, TILES):
-                row_maximum(step)
-            if in_range(step - 4, TILES):
-                quantised(step - 4)
-            if in_range(step - 1, TILES):
-                exponentials(step - 1)
+                window_maximum(step)
             if in_range(step - 3, TILES):
-                regrouped(step - 3)
-            if in_range(step - FIRST_V_STEP, BLOCKS // V_GROUP):
-                v_quantised(step - FIRST_V_STEP)
+                quantised(step - 3)
+            if in_range(step, TILES):
+                row_maximum(step)
+                exponentials(step)
+            if in_range(step - 1, TILES):
+                transposed(step - 1)
             if r == 0 and in_range(n + 1, BLOCKS):
-                kq_transposed(n + 1)
-            if r == 1 and in_range(n + 1, BLOCKS):
-                kq_copied(n + 1)
-            if r == 2 and in_range(n - 1, BLOCKS):
-                row_sums(n - 1)
-            if r == 2 and in_range(n - 2, BLOCKS):
-                product(n - 2)
-            if r == 3 and in_range(n + 1, BLOCKS):
-                diagonal_scores(n + 1)
-            if r == 3 and in_range(n - 2, BLOCKS):
+                prepare_qk(n + 1)
+            if r == 0 and in_range(n - 1, BLOCKS):
+                v_quantised(n - 1)
+            if r == 0 and in_range(n - 2, BLOCKS):
                 normalised(n - 2)
+            if r == 1 and in_range(n + 1, BLOCKS):
+                diagonal_scores(n + 1)
+            if r == 1 and in_range(n - 1, BLOCKS):
+                row_sums(n - 1)
+            if r == 2 and in_range(n + 1, BLOCKS):
+                diagonal_max(n + 1)
+            if r == 2 and in_range(n - 1, BLOCKS):
+                reciprocals(n - 1)
+            if r == 3 and in_range(n, BLOCKS):
+                v_regrouped(n)
+            if r == 3 and in_range(n - 1, BLOCKS):
+                product(n - 1)

from contextlib import ExitStack

import concourse.mybir as mybir
from concourse.masks import make_identity

F32 = mybir.dt.float32
BF16 = mybir.dt.bfloat16
U32 = mybir.dt.uint32
U8 = mybir.dt.uint8
FP8X4 = mybir.dt.float8_e4m3fn_x4
ALU = mybir.AluOpType
ACT = mybir.ActivationFunctionType
AXIS = mybir.AxisListType

P = 128
S = 4096
D = 128
PACK = 4
BLOCK = PACK * P
TILES = S // P
BLOCKS = S // BLOCK
SCALE = D ** -0.5
MASKED = -3.0e38

FLOPS = 2 * (2 * BLOCKS - 1) * 2 * BLOCK * BLOCK * D


def tile_exactslidingwindowattention_kernel(tc, q, k, v, out):
    nc = tc.nc
    q_blocks = q.flatten_outer_dims().rearrange("(n t p) d -> n p t d", t=PACK, p=P)
    k_blocks = k.flatten_outer_dims().rearrange("(n t p) d -> n p t d", t=PACK, p=P)
    v_blocks = v.flatten_outer_dims().rearrange("(n u p e) d -> n p u (e d)", u=2, p=P, e=2)
    out_blocks = out.flatten_outer_dims().rearrange("(n t p) d -> n p t d", t=PACK, p=P)

    with ExitStack() as ctx:
        ctx.enter_context(tc.manual_schedule())
        keep = ctx.enter_context(tc.tile_pool(name="keep", bufs=1))
        work = ctx.enter_context(tc.tile_pool(name="work", bufs=4))
        per_block = ctx.enter_context(tc.tile_pool(name="per_block", bufs=2))
        small = ctx.enter_context(tc.tile_pool(name="small", bufs=4))
        psum_window = ctx.enter_context(tc.psum_pool(name="psum_window", bufs=2))
        psum_diag = ctx.enter_context(tc.psum_pool(name="psum_diag", bufs=2))
        psum_eT = ctx.enter_context(tc.psum_pool(name="psum_eT", bufs=2))
        psum_num = ctx.enter_context(tc.psum_pool(name="psum_num", bufs=1))
        psum_qkT = ctx.enter_context(tc.psum_pool(name="psum_qkT", bufs=1))

        q_sb = keep.tile([P, BLOCKS, PACK, D], BF16)
        k_sb = keep.tile([P, BLOCKS, PACK, D], BF16)
        v_sb = keep.tile([P, BLOCKS, PACK, D], BF16)

        def load_v(n):
            nc.sync.dma_start(out=v_sb[:, n].rearrange("p (u e) d -> p u (e d)", u=2),
                              in_=v_blocks[n])

        for n in range(BLOCKS):
            nc.sync.dma_start(out=k_sb[:, n], in_=k_blocks[n])
            nc.sync.dma_start(out=q_sb[:, n], in_=q_blocks[n])
            if n > 0:
                load_v(n - 1)
        load_v(BLOCKS - 1)

        e_win = []
        for r in range(PACK):
            e_win_r = keep.tile([P, 2 * BLOCK], BF16, name="e_win%d" % r)
            nc.vector.memset(e_win_r[:], 0.0)
            e_win.append(e_win_r)
        den_parts = keep.tile([P, BLOCKS, PACK, 2], F32)
        nc.vector.memset(den_parts[:], 0.0)

        ident = keep.tile([P, P], BF16)
        make_identity(nc, ident[:])
        ident_f32 = keep.tile([P, P], F32)
        make_identity(nc, ident_f32[:])
        mask_own_f32 = keep.tile([P, P], F32)
        nc.gpsimd.memset(mask_own_f32[:], 0.0)
        nc.gpsimd.affine_select(
            out=mask_own_f32[:], in_=mask_own_f32[:], compare_op=ALU.is_ge, fill=MASKED,
            base=0, pattern=[[-1, P]], channel_multiplier=1,
        )
        mask_prev_f32 = keep.tile([P, P], F32)
        nc.gpsimd.memset(mask_prev_f32[:], 0.0)
        nc.gpsimd.affine_select(
            out=mask_prev_f32[:], in_=mask_prev_f32[:], compare_op=ALU.is_ge, fill=MASKED,
            base=-1, pattern=[[1, P]], channel_multiplier=-1,
        )
        mask_own = keep.tile([P, P], BF16)
        nc.vector.tensor_copy(out=mask_own[:], in_=mask_own_f32[:])
        mask_prev = keep.tile([P, P], BF16)
        nc.vector.tensor_copy(out=mask_prev[:], in_=mask_prev_f32[:])

        kqT = keep.tile([D, 2, S], BF16)
        kT = kqT[:, 0, :]
        qT = kqT[:, 1, :]
        v_codes = keep.tile([P, BLOCKS, D], U32, align_bytes=64)
        v_scales = keep.tile([P, BLOCKS, D], U8, align_bytes=64)

        diag_ps = {}
        diag_max = {}
        window_ps = {}
        window_max = {}
        neg_max = {}
        v_grouped = {}
        den = {}
        inv_den = {}
        num_ps = {}
        grouped = {}
        e_codes = {}
        e_scales = {}

        def first_key_tile(T):
            return max(T - PACK, 0)

        def first_side(n):
            return 0 if n > 0 else 1

        def prepare_qk(n):
            kqT_ps = psum_qkT.tile([D, 2, PACK, P], BF16)
            for t in range(PACK):
                nc.tensor.transpose(kqT_ps[:, 0, t, :], k_sb[:, n, t, :], ident[:])
            for t in range(PACK):
                nc.tensor.transpose(kqT_ps[:, 1, t, :], q_sb[:, n, t, :], ident[:])
            nc.scalar.copy(out=kqT[:, :, n * BLOCK:(n + 1) * BLOCK],
                           in_=kqT_ps[:].rearrange("d h t p -> d h (t p)"))

        def v_regrouped(n):
            v_grouped[n] = work.tile([P, D, PACK], BF16, name="v_grouped", align_bytes=64)
            nc.vector.tensor_copy(out=v_grouped[n][:], in_=v_sb[:, n].rearrange("p t d -> p d t"))

        def v_quantised(n):
            nc.vector.quantize_mx(
                out=v_codes[:, n, :].bitcast(FP8X4),
                scales=v_scales[:, n, :],
                in_=v_grouped[n][:].rearrange("p d t -> p (d t)"),
            )

        def diagonal_scores(n):
            diag_ps[n] = psum_diag.tile([P, PACK, P], F32, name="diag_ps")
            for r in range(PACK):
                tile_cols = slice((n * PACK + r) * P, (n * PACK + r + 1) * P)
                nc.tensor.matmul(out=diag_ps[n][:, r, :], lhsT=qT[:, tile_cols],
                                 rhs=kT[:, tile_cols], start=True, stop=False)
                nc.tensor.matmul(out=diag_ps[n][:, r, :], lhsT=ident[:], rhs=mask_own[:],
                                 start=False, stop=True)

        def diagonal_max(n):
            diag_max[n] = small.tile([P, PACK], F32, name="diag_max")
            nc.vector.tensor_reduce(out=diag_max[n][:], in_=diag_ps[n][:], axis=AXIS.X, op=ALU.max)

        def window_scores(T):
            if T == 0:
                return
            window_ps[T] = psum_window.tile([P, BLOCK], F32, name="window_ps")
            clipped = T >= PACK
            nc.tensor.matmul(out=window_ps[T][:, 0:(T - first_key_tile(T)) * P],
                             lhsT=qT[:, T * P:(T + 1) * P],
                             rhs=kT[:, first_key_tile(T) * P:T * P],
                             start=True, stop=not clipped)
            if clipped:
                nc.tensor.matmul(out=window_ps[T][:, 0:P], lhsT=ident[:], rhs=mask_prev[:],
                                 start=False, stop=True)

        def window_maximum(T):
            if T > 0:
                window_max[T] = small.tile([P, 1], F32, name="window_max")
                nc.vector.tensor_reduce(out=window_max[T][:],
                                        in_=window_ps[T][:, 0:(T - first_key_tile(T)) * P],
                                        axis=AXIS.X, op=ALU.max)

        def row_maximum(T):
            n, r = divmod(T, PACK)
            neg_max[T] = small.tile([P, 1], F32, name="neg_max")
            if T > 0:
                nc.vector.tensor_scalar(out=neg_max[T][:], in0=window_max[T][:],
                                        scalar1=diag_max[n][:, r:r + 1], scalar2=-SCALE,
                                        op0=ALU.max, op1=ALU.mult)
            else:
                nc.vector.tensor_scalar(out=neg_max[T][:], in0=diag_max[n][:, r:r + 1],
                                        scalar1=-SCALE, scalar2=None, op0=ALU.mult)

        def exponentials(T):
            n, r = divmod(T, PACK)
            width = (T - first_key_tile(T)) * P
            base = (first_key_tile(T) - (n - 1) * PACK) * P
            if T > 0:
                nc.scalar.activation(out=e_win[r][:, base:base + width],
                                     in_=window_ps[T][:, 0:width],
                                     func=ACT.Exp, bias=neg_max[T][:], scale=SCALE,
                                     accum_out=den_parts[:, n, r, 0:1])
            nc.scalar.activation(out=e_win[r][:, base + width:base + width + P],
                                 in_=diag_ps[n][:, r, :],
                                 func=ACT.Exp, bias=neg_max[T][:], scale=SCALE,
                                 accum_out=den_parts[:, n, r, 1:2])

        def transposed(T):
            n, r = divmod(T, PACK)
            eT_ps = psum_eT.tile([P, 2, 2, P], F32)
            words = e_win[r][:].bitcast(F32)
            for side in range(first_side(n), 2):
                for u in range(2):
                    c = (2 * side + u) * P
                    nc.tensor.transpose(eT_ps[:, side, u, :], words[:, c:c + P], ident_f32[:])
            grouped[T] = work.tile([P, 2, P, PACK], BF16, name="grouped", align_bytes=64)
            nc.scalar.copy(
                out=grouped[T][:].rearrange("p s q t -> p (s q t)").bitcast(F32).rearrange(
                    "p (s q u) -> p s q u", s=2, u=2)[:, first_side(n):],
                in_=eT_ps[:, first_side(n):].rearrange("p s u q -> p s q u"))

        def quantised(T):
            n, r = divmod(T, PACK)
            if r == 0:
                e_codes[n] = per_block.tile([P, PACK, 2 * P], U32, name="e_codes", align_bytes=64)
                e_scales[n] = per_block.tile([P, PACK, 2 * P], U8, name="e_scales", align_bytes=64)
            nc.vector.quantize_mx(
                out=e_codes[n][:, r, first_side(n) * P:].bitcast(FP8X4),
                scales=e_scales[n][:, r, first_side(n) * P:],
                in_=grouped[T][:, first_side(n):, :, :].rearrange("p s q t -> p (s q t)"),
            )

        def product(n):
            num_ps[n] = psum_num.tile([P, PACK, D], F32, name="num_ps")
            for r in range(PACK):
                for side in range(first_side(n), 2):
                    cols = slice(side * P, (side + 1) * P)
                    nc.tensor.matmul_mx(
                        out=num_ps[n][:, r, :],
                        lhsT=e_codes[n][:, r, cols].bitcast(FP8X4),
                        lhsT_scale=e_scales[n][:, r, cols],
                        rhs=v_codes[:, n - 1 + side, :].bitcast(FP8X4),
                        rhs_scale=v_scales[:, n - 1 + side, :],
                        start=(side == first_side(n)),
                        stop=(side == 1),
                    )

        def row_sums(n):
            den[n] = small.tile([P, PACK], F32, name="den")
            nc.vector.tensor_reduce(out=den[n][:], in_=den_parts[:, n], axis=AXIS.X, op=ALU.add)

        def reciprocals(n):
            inv_den[n] = small.tile([P, PACK], F32, name="inv_den")
            nc.vector.reciprocal(out=inv_den[n][:], in_=den[n][:])

        def normalised(n):
            out_sb = per_block.tile([P, PACK, D], F32)
            nc.vector.tensor_tensor(out=out_sb[:], in0=num_ps[n][:],
                                    in1=inv_den[n][:].unsqueeze(2).to_broadcast([P, PACK, D]),
                                    op=ALU.mult)
            nc.sync.dma_start(out=out_blocks[n], in_=out_sb[:])

        def in_range(x, count):
            return 0 <= x < count

        prepare_qk(0)
        diagonal_scores(0)
        diagonal_max(0)
        for step in range(-1, TILES + 2 * PACK + 1):
            n, r = divmod(step, PACK)
            if in_range(step + 1, TILES):
                window_scores(step + 1)
            if in_range(step, TILES):
                window_maximum(step)
            if in_range(step - 3, TILES):
                quantised(step - 3)
            if in_range(step, TILES):
                row_maximum(step)
                exponentials(step)
            if in_range(step - 1, TILES):
                transposed(step - 1)
            if r == 0 and in_range(n + 1, BLOCKS):
                prepare_qk(n + 1)
            if r == 0 and in_range(n - 1, BLOCKS):
                v_quantised(n - 1)
            if r == 0 and in_range(n - 2, BLOCKS):
                normalised(n - 2)
            if r == 1 and in_range(n + 1, BLOCKS):
                diagonal_scores(n + 1)
            if r == 1 and in_range(n - 1, BLOCKS):
                row_sums(n - 1)
            if r == 2 and in_range(n + 1, BLOCKS):
                diagonal_max(n + 1)
            if r == 2 and in_range(n - 1, BLOCKS):
                reciprocals(n - 1)
            if r == 3 and in_range(n, BLOCKS):
                v_regrouped(n)
            if r == 3 and in_range(n - 1, BLOCKS):
                product(n - 1)
